import numpy as np
import ml_dtypes


def mxq(x, axis, fmt="e4m3"):
    dtype, down = {"e4m3": (ml_dtypes.float8_e4m3fn, 7), "e5m2": (ml_dtypes.float8_e5m2, 14)}[fmt]
    v = np.moveaxis(np.asarray(x, np.float32).astype(ml_dtypes.bfloat16).astype(np.float64), axis, -1)
    blocks = v.reshape(v.shape[:-1] + (-1, 32))
    amax = np.abs(blocks).max(-1, keepdims=True)
    byte = np.maximum(np.where(amax > 0, np.frexp(amax)[1] - 1 + 127, 0) - down, 1)
    scale = np.exp2(byte - 127.0)
    codes = (blocks / scale).astype(np.float32).astype(dtype).astype(np.float64)
    return np.moveaxis((codes * scale).reshape(v.shape), -1, axis)


WIDE = False


def mx_kscale(k):
    if not WIDE:
        return np.ones(k)
    levels = np.array([10, -10, 5, -5, 0])
    a = np.random.permutation(np.resize(levels, k // 512 * 4)).reshape(k // 512, 4)
    idx = np.arange(k)
    return np.exp2(a[idx // 512, idx % 128 // 32])


BF16 = ml_dtypes.bfloat16


def bf(x):
    return np.asarray(x, np.float32).astype(BF16)


def f64(x):
    return np.asarray(x).astype(np.float64)


E2M1 = np.array([0.0, 0.5, 1.0, 1.5, 2.0, 3.0, 4.0, 6.0, -0.0, -0.5, -1.0, -1.5, -2.0, -3.0, -4.0, -6.0])


def pack_weight(w, fmt):
    k, n = w.shape
    w = f64(bf(w)).reshape(k // 32, 32, n)
    amax = np.abs(w).max(1)
    if fmt == "e4m3":
        byte = np.frexp(amax)[1] - 1 + 127 - 7
    else:
        mant, ex = np.frexp(amax / 6.0)
        byte = np.where(mant > 0.5, ex, ex - 1) + 127
    byte = np.clip(np.where(amax > 0, byte, 1), 1, 254)
    scaled = (w * np.exp2(127.0 - byte)[:, None, :]).reshape(k, n).astype(np.float32)
    by_word = np.ascontiguousarray(scaled.reshape(k // 512, 128, 4, n).transpose(0, 1, 3, 2))
    if fmt == "e4m3":
        words = by_word.astype(ml_dtypes.float8_e4m3fn).view(np.uint8)
    else:
        c = by_word.astype(ml_dtypes.float4_e2m1fn).view(np.uint8) & 0xF
        words = c[..., 0::2] | (c[..., 1::2] << 4)
    return np.ascontiguousarray(words), np.ascontiguousarray(byte.astype(np.uint8).reshape(k // 512, 16, n))


def unpack_weight(words, scales, fmt):
    g, p, n, _ = words.shape
    if fmt == "e4m3":
        vals = np.ascontiguousarray(words).view(ml_dtypes.float8_e4m3fn).astype(np.float64)
    else:
        nib = np.empty((g, p, n, 4), np.uint8)
        nib[..., 0::2] = words & 0xF
        nib[..., 1::2] = words >> 4
        vals = E2M1[nib]
    vals = vals * np.repeat(np.exp2(scales.astype(np.float64) - 127.0), 8, axis=1)[..., None]
    return vals.transpose(0, 1, 3, 2).reshape(g * 512, n)

def pack4(w):
    words, scales = pack_weight(w, "e2m1")
    return words.reshape(words.shape[0], 128, -1), scales


def unpack4(words, scales):
    return unpack_weight(words.reshape(words.shape[0], 128, -1, 2), scales, "e2m1")


B, CIN, P, COUT, W, H, HEADS = 2, 1024, 512, 2048, 16, 32, 4
N = W * H
EPS = 1e-5


def bn(y, g, b, m, v):
    return (y - f64(m)[None, :, None]) * (f64(g) / np.sqrt(f64(v) + EPS))[None, :, None] + f64(b)[None, :, None]


def setup_inputs():
    s, t = mx_kscale(P), mx_kscale(CIN)
    inp = {}
    inp["h_attn"] = bf(np.maximum(np.random.standard_normal((B, P, N)), 0.0) * s[None, :, None])
    inp["x"] = bf(np.random.standard_normal((B, CIN, N)) * t[None, :, None])
    conv3_w = np.random.standard_normal((COUT, P)) * 1.5 / np.sqrt(P) / s[None, :]
    inp["conv3_w_words"], inp["conv3_w_scales"] = pack4(conv3_w.T)
    inp["bn3_g"] = bf(np.random.uniform(0.5, 1.5, COUT))
    inp["bn3_b"] = bf(np.random.standard_normal(COUT) * 0.3)
    inp["bn3_m"] = bf(np.random.standard_normal(COUT) * 0.3)
    inp["bn3_v"] = bf(np.random.uniform(0.5, 1.5, COUT))
    sc_w = np.random.standard_normal((COUT, CIN)) / np.sqrt(CIN) / t[None, :]
    inp["sc_w_words"], inp["sc_w_scales"] = pack4(sc_w.T)
    inp["sc_b"] = bf(np.random.standard_normal(COUT) * 0.3)
    inp["scbn_g"] = bf(np.random.uniform(0.5, 1.5, COUT))
    inp["scbn_b"] = bf(np.random.standard_normal(COUT) * 0.3)
    inp["scbn_m"] = bf(np.random.standard_normal(COUT) * 0.3)
    inp["scbn_v"] = bf(np.random.uniform(0.5, 1.5, COUT))
    return inp


def reference(h_attn, x, conv3_w_words, conv3_w_scales, bn3_g, bn3_b, bn3_m, bn3_v, sc_w_words, sc_w_scales, sc_b, scbn_g, scbn_b, scbn_m, scbn_v):
    main = bn(unpack4(conv3_w_words, conv3_w_scales).T @ mxq(f64(h_attn), 1, "e4m3"), bn3_g, bn3_b, bn3_m, bn3_v)
    short = (unpack4(sc_w_words, sc_w_scales).T @ mxq(f64(x), 1, "e4m3")) + f64(sc_b)[None, :, None]
    short = bn(short, scbn_g, scbn_b, scbn_m, scbn_v)
    return np.maximum(main + short, 0.0)

@@ -1,0 +1,235 @@
+from contextlib import ExitStack
+
+import concourse.mybir as mybir
+from concourse.masks import make_identity
+
+BF16 = mybir.dt.bfloat16
+F32 = mybir.dt.float32
+I32 = mybir.dt.int32
+U8 = mybir.dt.uint8
+U32 = mybir.dt.uint32
+FP8X4 = mybir.dt.float8_e4m3fn_x4
+FP4X4 = mybir.dt.float4_e2m1fn_x4
+ALU = mybir.AluOpType
+ACT = mybir.ActivationFunctionType
+AXIS = mybir.AxisListType
+
+P = 128
+PACK = 4
+BATCH = 2
+N = 512
+COUT = 2048
+CO_TILES = COUT // P
+X_GROUPS = 2
+PASSES = 1 + X_GROUPS
+EPS = 1e-5
+FLT_MAX = 3.4028234663852886e38
+
+W3_CHUNKS = 2
+WSC_CHUNKS = 4
+LEAD = 8
+ACC_BUFS = 10
+VECTOR_COLS = 256
+
+FLOPS = 2 * BATCH * COUT * N * (512 + 1024)
+
+
+def tile_bottleneck_transformer_pb_kernel(
+    tc,
+    h_attn,
+    x,
+    conv3_w_words,
+    conv3_w_scales,
+    bn3_g,
+    bn3_b,
+    bn3_m,
+    bn3_v,
+    sc_w_words,
+    sc_w_scales,
+    sc_b,
+    scbn_g,
+    scbn_b,
+    scbn_m,
+    scbn_v,
+    out,
+):
+    nc = tc.nc
+    with ExitStack() as pools:
+        keep = pools.enter_context(tc.tile_pool(name="keep", bufs=1))
+        stage = pools.enter_context(tc.tile_pool(name="stage", bufs=3))
+        accs = pools.enter_context(tc.tile_pool(name="accs", bufs=ACC_BUFS))
+        psum_main = pools.enter_context(tc.psum_pool(name="psum_main", bufs=4))
+        psum_short = pools.enter_context(tc.psum_pool(name="psum_short", bufs=4))
+
+        raw = {}
+        codes = {}
+        planes = {}
+        for b in range(BATCH):
+            for c in range(PASSES):
+                raw[(b, c)] = keep.tile([P, PACK, N], BF16, name="raw%d%d" % (b, c))
+                codes[(b, c)] = keep.tile([P, N], U32, name="codes%d%d" % (b, c), align_bytes=64)
+                planes[(b, c)] = keep.tile([P, N], U8, name="planes%d%d" % (b, c), align_bytes=64)
+        w3_cols = COUT // W3_CHUNKS
+        wsc_cols = COUT // WSC_CHUNKS
+        w3_words = [
+            keep.tile([P, 2 * w3_cols], U8, name="w3_words%d" % i, align_bytes=64) for i in range(W3_CHUNKS)
+        ]
+        wsc_words = [
+            keep.tile([P, X_GROUPS, 2 * wsc_cols], U8, name="wsc_words%d" % i, align_bytes=64)
+            for i in range(WSC_CHUNKS)
+        ]
+        w3_plane = keep.tile([P, COUT], U8, name="w3_plane", align_bytes=64)
+        wsc_planes = keep.tile([P, X_GROUPS, COUT], U8, name="wsc_planes", align_bytes=64)
+
+        bn_rows = keep.tile([P, 2 * P], BF16, name="bn_rows")
+        ident = keep.tile([P, P], BF16, name="ident")
+        eps_col = keep.tile([P, 1], F32, name="eps_col")
+        warm = keep.tile([P, 1], F32, name="warm")
+
+        nc.vector.memset(bn_rows[64:P, :], 0.0)
+        nc.vector.memset(eps_col[:], EPS)
+        nc.vector.memset(w3_plane[:].bitcast(I32), 0)
+        nc.vector.memset(wsc_planes[:].rearrange("p g n -> p (g n)").bitcast(I32), 0)
+        nc.scalar.activation(out=warm[:], in_=eps_col[:], func=ACT.Sqrt)
+
+        bn_vectors = [bn3_v, scbn_v, bn3_g, scbn_g, bn3_m, scbn_m, bn3_b, scbn_b, sc_b]
+        for v, vector in enumerate(bn_vectors):
+            queue = nc.sync if v < 7 else nc.gpsimd
+            queue.dma_start(out=bn_rows[8 * v : 8 * v + 8, :], in_=vector.rearrange("(r c) -> r c", c=2 * P))
+        make_identity(nc, ident[:])
+
+        def load_activations(queue, b):
+            queue.dma_start(out=raw[(b, 0)][:], in_=h_attn[b].rearrange("(p t) n -> p t n", t=PACK))
+
+        def load_x(queue, b):
+            for g in range(X_GROUPS):
+                queue.dma_start(
+                    out=raw[(b, 1 + g)][:],
+                    in_=x[b, 512 * g : 512 * (g + 1), :].rearrange("(p t) n -> p t n", t=PACK),
+                )
+
+        def load_w3(i):
+            nc.sync.dma_start(
+                out=w3_words[i][:].bitcast(I32),
+                in_=conv3_w_words[0, :, 2 * w3_cols * i : 2 * w3_cols * (i + 1)].bitcast(I32),
+            )
+
+        def load_wsc(i):
+            nc.sync.dma_start(
+                out=wsc_words[i][:].bitcast(I32),
+                in_=sc_w_words[:, :, 2 * wsc_cols * i : 2 * wsc_cols * (i + 1)]
+                .rearrange("g p w -> p g w")
+                .bitcast(I32),
+            )
+
+        load_activations(nc.scalar, 0)
+        for q in range(4):
+            nc.sync.dma_start(
+                out=w3_plane[32 * q : 32 * q + 4, :].bitcast(I32),
+                in_=conv3_w_scales[0, 4 * q : 4 * q + 4, :].bitcast(I32),
+            )
+        load_w3(0)
+        load_x(nc.scalar, 0)
+        load_wsc(0)
+        for q in range(4):
+            nc.sync.dma_start(
+                out=wsc_planes[32 * q : 32 * q + 4, :, :].bitcast(I32),
+                in_=sc_w_scales[:, 4 * q : 4 * q + 4, :].rearrange("g r n -> r g n").bitcast(I32),
+            )
+        load_w3(1)
+        load_wsc(1)
+        load_activations(nc.sync, 1)
+        load_x(nc.sync, 1)
+        load_wsc(2)
+        load_wsc(3)
+
+        bn_ps = psum_main.tile([P, 2, P], BF16, tag="main", name="bn_ps")
+        for h in range(2):
+            nc.tensor.transpose(bn_ps[:, h, :], bn_rows[:, P * h : P * (h + 1)], ident[:])
+        bn = keep.tile([P, 9, 8, 2], F32, name="bn")
+        nc.vector.tensor_copy(out=bn[:], in_=bn_ps[:, :, 0:72].rearrange("p h (v r) -> p v r h", v=9))
+        by_tile = bn[:].rearrange("p v r h -> p v (r h)")
+        rstd = keep.tile([P, 2, CO_TILES], F32, name="rstd")
+        slope = keep.tile([P, 2, CO_TILES], F32, name="slope")
+        terms = keep.tile([P, 3, CO_TILES], F32, name="terms")
+        shift = keep.tile([P, CO_TILES], F32, name="shift")
+        nc.scalar.activation(out=rstd[:], in_=by_tile[:, 0:2, :], func=ACT.Sqrt, bias=eps_col[:, 0:1])
+        nc.vector.tensor_scalar_mul(out=by_tile[:, 4, :], in0=by_tile[:, 4, :], scalar1=-1.0)
+        nc.vector.tensor_sub(out=by_tile[:, 5, :], in0=by_tile[:, 8, :], in1=by_tile[:, 5, :])
+        nc.vector.tensor_add(out=terms[:, 2, :], in0=by_tile[:, 6, :], in1=by_tile[:, 7, :])
+        nc.vector.reciprocal(out=rstd[:], in_=rstd[:])
+        nc.vector.tensor_mul(out=slope[:], in0=by_tile[:, 2:4, :], in1=rstd[:])
+        nc.vector.tensor_mul(out=terms[:, 0:2, :], in0=by_tile[:, 4:6, :], in1=slope[:])
+        nc.vector.reduce_sum(out=shift[:], in_=terms[:].rearrange("p v c -> p c v"), axis=AXIS.X)
+
+        for b in range(BATCH):
+            for c in range(PASSES):
+                grouped = stage.tile([P, N, PACK], BF16, name="grouped", align_bytes=64)
+                source = raw[(b, c)][:].rearrange("p t (c i) -> p c t i", i=4)
+                target = grouped[:].rearrange("p (c i) t -> p c t i", i=4)
+                split = VECTOR_COLS // 4
+                nc.vector.tensor_copy(out=target[:, 0:split], in_=source[:, 0:split])
+                nc.scalar.copy(out=target[:, split:], in_=source[:, split:])
+                nc.vector.quantize_mx(
+                    out=codes[(b, c)][:].bitcast(FP8X4),
+                    scales=planes[(b, c)][:],
+                    in_=grouped[:].rearrange("p n t -> p (n t)"),
+                )
+
+        tiles = [(b, ct) for b in range(BATCH) for ct in range(CO_TILES)]
+        acc_of = {}
+        for step in range(len(tiles) + LEAD):
+            if step < len(tiles):
+                b, ct = tiles[step]
+                if ct % 2 == 0:
+                    acc_of[(b, ct // 2)] = accs.tile([P, 2, N], F32, name="acc")
+                acc = acc_of[(b, ct // 2)]
+                chunk, col = divmod(ct * P, w3_cols)
+                main = psum_main.tile([P, N], F32, tag="main", name="main")
+                nc.tensor.matmul_mx(
+                    out=main[:],
+                    lhsT=w3_words[chunk][:, 2 * col : 2 * (col + P)].bitcast(FP4X4),
+                    lhsT_scale=w3_plane[:, ct * P : (ct + 1) * P],
+                    rhs=codes[(b, 0)][:].bitcast(FP8X4),
+                    rhs_scale=planes[(b, 0)][:],
+                    start=True,
+                    stop=True,
+                )
+                nc.scalar.activation(
+                    out=acc[:, ct % 2, :],
+                    in_=main[:],
+                    func=ACT.Identity,
+                    scale=slope[:, 0, ct : ct + 1],
+                    bias=shift[:, ct : ct + 1],
+                )
+            if step >= LEAD:
+                b, ct = tiles[step - LEAD]
+                acc = acc_of[(b, ct // 2)]
+                chunk, col = divmod(ct * P, wsc_cols)
+                short = psum_short.tile([P, N], F32, name="short")
+                for g in range(X_GROUPS):
+                    nc.tensor.matmul_mx(
+                        out=short[:],
+                        lhsT=wsc_words[chunk][:, g, 2 * col : 2 * (col + P)].bitcast(FP4X4),
+                        lhsT_scale=wsc_planes[:, g, ct * P : (ct + 1) * P],
+                        rhs=codes[(b, 1 + g)][:].bitcast(FP8X4),
+                        rhs_scale=planes[(b, 1 + g)][:],
+                        start=(g == 0),
+                        stop=(g == X_GROUPS - 1),
+                    )
+                nc.vector.scalar_tensor_tensor(
+                    out=acc[:, ct % 2, :],
+                    in0=short[:],
+                    scalar=slope[:, 1, ct : ct + 1],
+                    in1=acc[:, ct % 2, :],
+                    op0=ALU.mult,
+                    op1=ALU.add,
+                )
+                if ct % 2 == 1:
+                    nc.gpsimd.tensor_scalar(
+                        out=acc[:], in0=acc[:], scalar1=FLT_MAX, scalar2=0.0, op0=ALU.min, op1=ALU.max
+                    )
+                    nc.sync.dma_start(
+                        out=out[b, (ct - 1) * P : (ct + 1) * P, :].rearrange("(j p) n -> p j n", p=P),
+                        in_=acc[:],
+                    )

@@ -27,8 +27,8 @@ FLT_MAX = 3.4028234663852886e38
 
 W3_CHUNKS = 2
 WSC_CHUNKS = 4
-LEAD = 8
-ACC_BUFS = 10
+LEAD = 12
+ACC_BUFS = 16
 VECTOR_COLS = 256
 
 FLOPS = 2 * BATCH * COUT * N * (512 + 1024)
@@ -58,8 +58,7 @@ def tile_bottleneck_transformer_pb_kernel(
         keep = pools.enter_context(tc.tile_pool(name="keep", bufs=1))
         stage = pools.enter_context(tc.tile_pool(name="stage", bufs=3))
         accs = pools.enter_context(tc.tile_pool(name="accs", bufs=ACC_BUFS))
-        psum_main = pools.enter_context(tc.psum_pool(name="psum_main", bufs=4))
-        psum_short = pools.enter_context(tc.psum_pool(name="psum_short", bufs=4))
+        psum = pools.enter_context(tc.psum_pool(name="psum", bufs=8))
 
         raw = {}
         codes = {}
@@ -143,7 +142,7 @@ def tile_bottleneck_transformer_pb_kernel(
         load_wsc(2)
         load_wsc(3)
 
-        bn_ps = psum_main.tile([P, 2, P], BF16, tag="main", name="bn_ps")
+        bn_ps = psum.tile([P, 2, P], BF16, tag="bank", name="bn_ps")
         for h in range(2):
             nc.tensor.transpose(bn_ps[:, h, :], bn_rows[:, P * h : P * (h + 1)], ident[:])
         bn = keep.tile([P, 9, 8, 2], F32, name="bn")
@@ -162,30 +161,41 @@ def tile_bottleneck_transformer_pb_kernel(
         nc.vector.tensor_mul(out=terms[:, 0:2, :], in0=by_tile[:, 4:6, :], in1=slope[:])
         nc.vector.reduce_sum(out=shift[:], in_=terms[:].rearrange("p v c -> p c v"), axis=AXIS.X)
 
-        for b in range(BATCH):
-            for c in range(PASSES):
-                grouped = stage.tile([P, N, PACK], BF16, name="grouped", align_bytes=64)
-                source = raw[(b, c)][:].rearrange("p t (c i) -> p c t i", i=4)
-                target = grouped[:].rearrange("p (c i) t -> p c t i", i=4)
-                split = VECTOR_COLS // 4
-                nc.vector.tensor_copy(out=target[:, 0:split], in_=source[:, 0:split])
-                nc.scalar.copy(out=target[:, split:], in_=source[:, split:])
-                nc.vector.quantize_mx(
-                    out=codes[(b, c)][:].bitcast(FP8X4),
-                    scales=planes[(b, c)][:],
-                    in_=grouped[:].rearrange("p n t -> p (n t)"),
-                )
+        grouped_of = {}
+
+        def regroup(b, c):
+            grouped = stage.tile([P, N, PACK], BF16, name="grouped", align_bytes=64)
+            grouped_of[(b, c)] = grouped
+            source = raw[(b, c)][:].rearrange("p t (c i) -> p c t i", i=4)
+            target = grouped[:].rearrange("p (c i) t -> p c t i", i=4)
+            split = VECTOR_COLS // 4
+            nc.vector.tensor_copy(out=target[:, 0:split], in_=source[:, 0:split])
+            nc.scalar.copy(out=target[:, split:], in_=source[:, split:])
+
+        def quantise(b, c):
+            nc.vector.quantize_mx(
+                out=codes[(b, c)][:].bitcast(FP8X4),
+                scales=planes[(b, c)][:],
+                in_=grouped_of[(b, c)][:].rearrange("p n t -> p (n t)"),
+            )
+
+        for c in range(PASSES):
+            regroup(0, c)
+            quantise(0, c)
+        later = {9: (regroup, 0), 10: (quantise, 0), 12: (regroup, 1), 13: (quantise, 1), 15: (regroup, 2), 16: (quantise, 2)}
 
         tiles = [(b, ct) for b in range(BATCH) for ct in range(CO_TILES)]
         acc_of = {}
         for step in range(len(tiles) + LEAD):
+            if step in later:
+                later[step][0](1, later[step][1])
             if step < len(tiles):
                 b, ct = tiles[step]
                 if ct % 2 == 0:
                     acc_of[(b, ct // 2)] = accs.tile([P, 2, N], F32, name="acc")
                 acc = acc_of[(b, ct // 2)]
                 chunk, col = divmod(ct * P, w3_cols)
-                main = psum_main.tile([P, N], F32, tag="main", name="main")
+                main = psum.tile([P, N], F32, tag="bank", name="main")
                 nc.tensor.matmul_mx(
                     out=main[:],
                     lhsT=w3_words[chunk][:, 2 * col : 2 * (col + P)].bitcast(FP4X4),
@@ -195,18 +205,28 @@ def tile_bottleneck_transformer_pb_kernel(
                     start=True,
                     stop=True,
                 )
-                nc.scalar.activation(
-                    out=acc[:, ct % 2, :],
-                    in_=main[:],
-                    func=ACT.Identity,
-                    scale=slope[:, 0, ct : ct + 1],
-                    bias=shift[:, ct : ct + 1],
-                )
+                if step < LEAD and step % 2 == 1:
+                    nc.vector.tensor_scalar(
+                        out=acc[:, ct % 2, :],
+                        in0=main[:],
+                        scalar1=slope[:, 0, ct : ct + 1],
+                        scalar2=shift[:, ct : ct + 1],
+                        op0=ALU.mult,
+                        op1=ALU.add,
+                    )
+                else:
+                    nc.scalar.activation(
+                        out=acc[:, ct % 2, :],
+                        in_=main[:],
+                        func=ACT.Identity,
+                        scale=slope[:, 0, ct : ct + 1],
+                        bias=shift[:, ct : ct + 1],
+                    )
             if step >= LEAD:
                 b, ct = tiles[step - LEAD]
                 acc = acc_of[(b, ct // 2)]
                 chunk, col = divmod(ct * P, wsc_cols)
-                short = psum_short.tile([P, N], F32, name="short")
+                short = psum.tile([P, N], F32, tag="bank", name="short")
                 for g in range(X_GROUPS):
                     nc.tensor.matmul_mx(
                         out=short[:],
@@ -225,7 +245,10 @@ def tile_bottleneck_transformer_pb_kernel(
                     op0=ALU.mult,
                     op1=ALU.add,
                 )
-                if ct % 2 == 1:
+                if step >= len(tiles):
+                    nc.scalar.activation(out=acc[:, ct % 2, :], in_=acc[:, ct % 2, :], func=ACT.Relu)
+                    nc.sync.dma_start(out=out[b, ct * P : (ct + 1) * P, :], in_=acc[:, ct % 2, :])
+                elif ct % 2 == 1:
                     nc.gpsimd.tensor_scalar(
                         out=acc[:], in0=acc[:], scalar1=FLT_MAX, scalar2=0.0, op0=ALU.min, op1=ALU.max
                     )

@@ -27,7 +27,7 @@ FLT_MAX = 3.4028234663852886e38
 
 W3_CHUNKS = 2
 WSC_CHUNKS = 4
-LEAD = 12
+LEAD = 8
 ACC_BUFS = 16
 VECTOR_COLS = 256
 

@@ -182,7 +182,7 @@ def tile_bottleneck_transformer_pb_kernel(
         for c in range(PASSES):
             regroup(0, c)
             quantise(0, c)
-        later = {9: (regroup, 0), 10: (quantise, 0), 12: (regroup, 1), 13: (quantise, 1), 15: (regroup, 2), 16: (quantise, 2)}
+        later = {9: (regroup, 0), 10: (quantise, 0), 13: (regroup, 1), 14: (quantise, 1), 17: (regroup, 2), 18: (quantise, 2)}
 
         tiles = [(b, ct) for b in range(BATCH) for ct in range(CO_TILES)]
         acc_of = {}

@@ -149,17 +149,21 @@ def tile_bottleneck_transformer_pb_kernel(
         nc.vector.tensor_copy(out=bn[:], in_=bn_ps[:, :, 0:72].rearrange("p h (v r) -> p v r h", v=9))
         by_tile = bn[:].rearrange("p v r h -> p v (r h)")
         rstd = keep.tile([P, 2, CO_TILES], F32, name="rstd")
-        slope = keep.tile([P, 2, CO_TILES], F32, name="slope")
-        terms = keep.tile([P, 3, CO_TILES], F32, name="terms")
+        scaled = keep.tile([P, 5, CO_TILES], F32, name="scaled")
+        slope = scaled[:, 0:2, :]
         shift = keep.tile([P, CO_TILES], F32, name="shift")
         nc.scalar.activation(out=rstd[:], in_=by_tile[:, 0:2, :], func=ACT.Sqrt, bias=eps_col[:, 0:1])
         nc.vector.tensor_scalar_mul(out=by_tile[:, 4, :], in0=by_tile[:, 4, :], scalar1=-1.0)
         nc.vector.tensor_sub(out=by_tile[:, 5, :], in0=by_tile[:, 8, :], in1=by_tile[:, 5, :])
-        nc.vector.tensor_add(out=terms[:, 2, :], in0=by_tile[:, 6, :], in1=by_tile[:, 7, :])
+        nc.vector.tensor_add(out=scaled[:, 4, :], in0=by_tile[:, 6, :], in1=by_tile[:, 7, :])
+        nc.vector.tensor_mul(out=by_tile[:, 4:6, :], in0=by_tile[:, 4:6, :], in1=by_tile[:, 2:4, :])
         nc.vector.reciprocal(out=rstd[:], in_=rstd[:])
-        nc.vector.tensor_mul(out=slope[:], in0=by_tile[:, 2:4, :], in1=rstd[:])
-        nc.vector.tensor_mul(out=terms[:, 0:2, :], in0=by_tile[:, 4:6, :], in1=slope[:])
-        nc.vector.reduce_sum(out=shift[:], in_=terms[:].rearrange("p v c -> p c v"), axis=AXIS.X)
+        nc.vector.tensor_mul(
+            out=scaled[:, 0:4, :].rearrange("p (k v) c -> p k v c", k=2),
+            in0=by_tile[:, 2:6, :].rearrange("p (k v) c -> p k v c", k=2),
+            in1=rstd[:].unsqueeze(1).to_broadcast([P, 2, 2, CO_TILES]),
+        )
+        nc.vector.reduce_sum(out=shift[:], in_=scaled[:, 2:5, :].rearrange("p v c -> p c v"), axis=AXIS.X)
 
         grouped_of = {}
 

@@ -28,6 +28,7 @@ FLT_MAX = 3.4028234663852886e38
 W3_CHUNKS = 2
 WSC_CHUNKS = 4
 LEAD = 8
+SINGLES = 4
 ACC_BUFS = 16
 VECTOR_COLS = 256
 
@@ -186,77 +187,94 @@ def tile_bottleneck_transformer_pb_kernel(
         for c in range(PASSES):
             regroup(0, c)
             quantise(0, c)
-        later = {9: (regroup, 0), 10: (quantise, 0), 13: (regroup, 1), 14: (quantise, 1), 17: (regroup, 2), 18: (quantise, 2)}
+        later = {1: (regroup, 0), 2: (quantise, 0), 5: (regroup, 1), 6: (quantise, 1), 9: (regroup, 2), 10: (quantise, 2)}
 
         tiles = [(b, ct) for b in range(BATCH) for ct in range(CO_TILES)]
+        count = len(tiles)
         acc_of = {}
-        for step in range(len(tiles) + LEAD):
-            if step in later:
-                later[step][0](1, later[step][1])
-            if step < len(tiles):
-                b, ct = tiles[step]
-                if ct % 2 == 0:
-                    acc_of[(b, ct // 2)] = accs.tile([P, 2, N], F32, name="acc")
-                acc = acc_of[(b, ct // 2)]
-                chunk, col = divmod(ct * P, w3_cols)
-                main = psum.tile([P, N], F32, tag="bank", name="main")
-                nc.tensor.matmul_mx(
-                    out=main[:],
-                    lhsT=w3_words[chunk][:, 2 * col : 2 * (col + P)].bitcast(FP4X4),
-                    lhsT_scale=w3_plane[:, ct * P : (ct + 1) * P],
-                    rhs=codes[(b, 0)][:].bitcast(FP8X4),
-                    rhs_scale=planes[(b, 0)][:],
-                    start=True,
-                    stop=True,
-                )
-                if step < LEAD and step % 2 == 1:
-                    nc.vector.tensor_scalar(
-                        out=acc[:, ct % 2, :],
-                        in0=main[:],
-                        scalar1=slope[:, 0, ct : ct + 1],
-                        scalar2=shift[:, ct : ct + 1],
-                        op0=ALU.mult,
-                        op1=ALU.add,
-                    )
-                else:
-                    nc.scalar.activation(
-                        out=acc[:, ct % 2, :],
-                        in_=main[:],
-                        func=ACT.Identity,
-                        scale=slope[:, 0, ct : ct + 1],
-                        bias=shift[:, ct : ct + 1],
-                    )
-            if step >= LEAD:
-                b, ct = tiles[step - LEAD]
-                acc = acc_of[(b, ct // 2)]
-                chunk, col = divmod(ct * P, wsc_cols)
-                short = psum.tile([P, N], F32, tag="bank", name="short")
-                for g in range(X_GROUPS):
-                    nc.tensor.matmul_mx(
-                        out=short[:],
-                        lhsT=wsc_words[chunk][:, g, 2 * col : 2 * (col + P)].bitcast(FP4X4),
-                        lhsT_scale=wsc_planes[:, g, ct * P : (ct + 1) * P],
-                        rhs=codes[(b, 1 + g)][:].bitcast(FP8X4),
-                        rhs_scale=planes[(b, 1 + g)][:],
-                        start=(g == 0),
-                        stop=(g == X_GROUPS - 1),
-                    )
-                nc.vector.scalar_tensor_tensor(
+
+        def main_tile(i):
+            b, ct = tiles[i]
+            if ct % 2 == 0:
+                acc_of[(b, ct // 2)] = accs.tile([P, 2, N], F32, name="acc")
+            acc = acc_of[(b, ct // 2)]
+            chunk, col = divmod(ct * P, w3_cols)
+            main = psum.tile([P, N], F32, tag="bank", name="main")
+            nc.tensor.matmul_mx(
+                out=main[:],
+                lhsT=w3_words[chunk][:, 2 * col : 2 * (col + P)].bitcast(FP4X4),
+                lhsT_scale=w3_plane[:, ct * P : (ct + 1) * P],
+                rhs=codes[(b, 0)][:].bitcast(FP8X4),
+                rhs_scale=planes[(b, 0)][:],
+                start=True,
+                stop=True,
+            )
+            if i < LEAD and i % 2 == 1:
+                nc.vector.tensor_scalar(
                     out=acc[:, ct % 2, :],
-                    in0=short[:],
-                    scalar=slope[:, 1, ct : ct + 1],
-                    in1=acc[:, ct % 2, :],
+                    in0=main[:],
+                    scalar1=slope[:, 0, ct : ct + 1],
+                    scalar2=shift[:, ct : ct + 1],
                     op0=ALU.mult,
                     op1=ALU.add,
                 )
-                if step >= len(tiles):
+            else:
+                nc.scalar.activation(
+                    out=acc[:, ct % 2, :],
+                    in_=main[:],
+                    func=ACT.Identity,
+                    scale=slope[:, 0, ct : ct + 1],
+                    bias=shift[:, ct : ct + 1],
+                )
+
+        def short_tile(i):
+            b, ct = tiles[i]
+            acc = acc_of[(b, ct // 2)]
+            chunk, col = divmod(ct * P, wsc_cols)
+            short = psum.tile([P, N], F32, tag="bank", name="short")
+            for g in range(X_GROUPS):
+                nc.tensor.matmul_mx(
+                    out=short[:],
+                    lhsT=wsc_words[chunk][:, g, 2 * col : 2 * (col + P)].bitcast(FP4X4),
+                    lhsT_scale=wsc_planes[:, g, ct * P : (ct + 1) * P],
+                    rhs=codes[(b, 1 + g)][:].bitcast(FP8X4),
+                    rhs_scale=planes[(b, 1 + g)][:],
+                    start=(g == 0),
+                    stop=(g == X_GROUPS - 1),
+                )
+            nc.vector.scalar_tensor_tensor(
+                out=acc[:, ct % 2, :],
+                in0=short[:],
+                scalar=slope[:, 1, ct : ct + 1],
+                in1=acc[:, ct % 2, :],
+                op0=ALU.mult,
+                op1=ALU.add,
+            )
+            if i >= count - SINGLES:
+                if i == count - 1:
+                    nc.vector.tensor_scalar_max(out=acc[:, ct % 2, :], in0=acc[:, ct % 2, :], scalar1=0.0)
+                elif i == count - 2:
                     nc.scalar.activation(out=acc[:, ct % 2, :], in_=acc[:, ct % 2, :], func=ACT.Relu)
-                    nc.sync.dma_start(out=out[b, ct * P : (ct + 1) * P, :], in_=acc[:, ct % 2, :])
-                elif ct % 2 == 1:
+                else:
                     nc.gpsimd.tensor_scalar(
-                        out=acc[:], in0=acc[:], scalar1=FLT_MAX, scalar2=0.0, op0=ALU.min, op1=ALU.max
+                        out=acc[:, ct % 2, :], in0=acc[:, ct % 2, :], scalar1=FLT_MAX, scalar2=0.0, op0=ALU.min, op1=ALU.max
                     )
-                    nc.sync.dma_start(
-                        out=out[b, (ct - 1) * P : (ct + 1) * P, :].rearrange("(j p) n -> p j n", p=P),
-                        in_=acc[:],
-                    )
+                nc.sync.dma_start(out=out[b, ct * P : (ct + 1) * P, :], in_=acc[:, ct % 2, :])
+            elif ct % 2 == 1:
+                nc.gpsimd.tensor_scalar(
+                    out=acc[:], in0=acc[:], scalar1=FLT_MAX, scalar2=0.0, op0=ALU.min, op1=ALU.max
+                )
+                nc.sync.dma_start(
+                    out=out[b, (ct - 1) * P : (ct + 1) * P, :].rearrange("(j p) n -> p j n", p=P),
+                    in_=acc[:],
+                )
+
+        issued = 0
+        for s in range(count):
+            if s in later:
+                later[s][0](1, later[s][1])
+            lead = 2 + ((LEAD - 2) * (count - 1 - s)) // (count - 1)
+            while issued < min(count, s + lead):
+                main_tile(issued)
+                issued += 1
+            short_tile(s)

@@ -31,6 +31,7 @@ LEAD = 8
 SINGLES = 4
 ACC_BUFS = 16
 VECTOR_COLS = 256
+LATER_VECTOR_COLS = 128
 
 FLOPS = 2 * BATCH * COUT * N * (512 + 1024)
 
@@ -90,7 +91,7 @@ def tile_bottleneck_transformer_pb_kernel(
         nc.vector.memset(eps_col[:], EPS)
         nc.vector.memset(w3_plane[:].bitcast(I32), 0)
         nc.vector.memset(wsc_planes[:].rearrange("p g n -> p (g n)").bitcast(I32), 0)
-        nc.scalar.activation(out=warm[:], in_=eps_col[:], func=ACT.Sqrt)
+        nc.scalar.activation(out=warm[:], in_=eps_col[:], func=ACT.Abs_reciprocal_sqrt)
 
         bn_vectors = [bn3_v, scbn_v, bn3_g, scbn_g, bn3_m, scbn_m, bn3_b, scbn_b, sc_b]
         for v, vector in enumerate(bn_vectors):
@@ -147,24 +148,18 @@ def tile_bottleneck_transformer_pb_kernel(
         for h in range(2):
             nc.tensor.transpose(bn_ps[:, h, :], bn_rows[:, P * h : P * (h + 1)], ident[:])
         bn = keep.tile([P, 9, 8, 2], F32, name="bn")
-        nc.vector.tensor_copy(out=bn[:], in_=bn_ps[:, :, 0:72].rearrange("p h (v r) -> p v r h", v=9))
+        nc.scalar.copy(out=bn[:], in_=bn_ps[:, :, 0:72].rearrange("p h (v r) -> p v r h", v=9))
         by_tile = bn[:].rearrange("p v r h -> p v (r h)")
         rstd = keep.tile([P, 2, CO_TILES], F32, name="rstd")
-        scaled = keep.tile([P, 5, CO_TILES], F32, name="scaled")
-        slope = scaled[:, 0:2, :]
+        slope = keep.tile([P, 2, CO_TILES], F32, name="slope")
         shift = keep.tile([P, CO_TILES], F32, name="shift")
-        nc.scalar.activation(out=rstd[:], in_=by_tile[:, 0:2, :], func=ACT.Sqrt, bias=eps_col[:, 0:1])
-        nc.vector.tensor_scalar_mul(out=by_tile[:, 4, :], in0=by_tile[:, 4, :], scalar1=-1.0)
-        nc.vector.tensor_sub(out=by_tile[:, 5, :], in0=by_tile[:, 8, :], in1=by_tile[:, 5, :])
-        nc.vector.tensor_add(out=scaled[:, 4, :], in0=by_tile[:, 6, :], in1=by_tile[:, 7, :])
-        nc.vector.tensor_mul(out=by_tile[:, 4:6, :], in0=by_tile[:, 4:6, :], in1=by_tile[:, 2:4, :])
-        nc.vector.reciprocal(out=rstd[:], in_=rstd[:])
-        nc.vector.tensor_mul(
-            out=scaled[:, 0:4, :].rearrange("p (k v) c -> p k v c", k=2),
-            in0=by_tile[:, 2:6, :].rearrange("p (k v) c -> p k v c", k=2),
-            in1=rstd[:].unsqueeze(1).to_broadcast([P, 2, 2, CO_TILES]),
-        )
-        nc.vector.reduce_sum(out=shift[:], in_=scaled[:, 2:5, :].rearrange("p v c -> p c v"), axis=AXIS.X)
+        nc.scalar.activation(out=rstd[:], in_=by_tile[:, 0:2, :], func=ACT.Abs_reciprocal_sqrt, bias=eps_col[:, 0:1])
+        nc.gpsimd.tensor_sub(out=by_tile[:, 5, :], in0=by_tile[:, 8, :], in1=by_tile[:, 5, :])
+        nc.gpsimd.tensor_add(out=by_tile[:, 6, :], in0=by_tile[:, 6, :], in1=by_tile[:, 7, :])
+        nc.gpsimd.tensor_mul(out=slope[:], in0=by_tile[:, 2:4, :], in1=rstd[:])
+        nc.gpsimd.tensor_mul(out=by_tile[:, 4:6, :], in0=by_tile[:, 4:6, :], in1=slope[:])
+        nc.gpsimd.tensor_sub(out=by_tile[:, 6, :], in0=by_tile[:, 6, :], in1=by_tile[:, 4, :])
+        nc.gpsimd.tensor_add(out=shift[:], in0=by_tile[:, 6, :], in1=by_tile[:, 5, :])
 
         grouped_of = {}
 
@@ -173,7 +168,7 @@ def tile_bottleneck_transformer_pb_kernel(
             grouped_of[(b, c)] = grouped
             source = raw[(b, c)][:].rearrange("p t (c i) -> p c t i", i=4)
             target = grouped[:].rearrange("p (c i) t -> p c t i", i=4)
-            split = VECTOR_COLS // 4
+            split = (VECTOR_COLS if b == 0 else LATER_VECTOR_COLS) // 4
             nc.vector.tensor_copy(out=target[:, 0:split], in_=source[:, 0:split])
             nc.scalar.copy(out=target[:, split:], in_=source[:, split:])
 

@@ -29,6 +29,7 @@ W3_CHUNKS = 2
 WSC_CHUNKS = 4
 LEAD = 8
 SINGLES = 4
+SHORT_RELUS = 12
 ACC_BUFS = 16
 VECTOR_COLS = 256
 LATER_VECTOR_COLS = 128
@@ -255,6 +256,15 @@ def tile_bottleneck_transformer_pb_kernel(
                         out=acc[:, ct % 2, :], in0=acc[:, ct % 2, :], scalar1=FLT_MAX, scalar2=0.0, op0=ALU.min, op1=ALU.max
                     )
                 nc.sync.dma_start(out=out[b, ct * P : (ct + 1) * P, :], in_=acc[:, ct % 2, :])
+            elif i < SHORT_RELUS:
+                nc.gpsimd.tensor_scalar(
+                    out=acc[:, ct % 2, :], in0=acc[:, ct % 2, :], scalar1=FLT_MAX, scalar2=0.0, op0=ALU.min, op1=ALU.max
+                )
+                if ct % 2 == 1:
+                    nc.sync.dma_start(
+                        out=out[b, (ct - 1) * P : (ct + 1) * P, :].rearrange("(j p) n -> p j n", p=P),
+                        in_=acc[:],
+                    )
             elif ct % 2 == 1:
                 nc.gpsimd.tensor_scalar(
                     out=acc[:], in0=acc[:], scalar1=FLT_MAX, scalar2=0.0, op0=ALU.min, op1=ALU.max

from contextlib import ExitStack

import concourse.mybir as mybir
from concourse.masks import make_identity

BF16 = mybir.dt.bfloat16
F32 = mybir.dt.float32
I32 = mybir.dt.int32
U8 = mybir.dt.uint8
U32 = mybir.dt.uint32
FP8X4 = mybir.dt.float8_e4m3fn_x4
FP4X4 = mybir.dt.float4_e2m1fn_x4
ALU = mybir.AluOpType
ACT = mybir.ActivationFunctionType
AXIS = mybir.AxisListType

P = 128
PACK = 4
BATCH = 2
N = 512
COUT = 2048
CO_TILES = COUT // P
X_GROUPS = 2
PASSES = 1 + X_GROUPS
EPS = 1e-5
FLT_MAX = 3.4028234663852886e38

W3_CHUNKS = 2
WSC_CHUNKS = 4
LEAD = 8
SINGLES = 4
SHORT_RELUS = 12
ACC_BUFS = 16
VECTOR_COLS = 256
LATER_VECTOR_COLS = 128

FLOPS = 2 * BATCH * COUT * N * (512 + 1024)


def tile_bottleneck_transformer_pb_kernel(
    tc,
    h_attn,
    x,
    conv3_w_words,
    conv3_w_scales,
    bn3_g,
    bn3_b,
    bn3_m,
    bn3_v,
    sc_w_words,
    sc_w_scales,
    sc_b,
    scbn_g,
    scbn_b,
    scbn_m,
    scbn_v,
    out,
):
    nc = tc.nc
    with ExitStack() as pools:
        keep = pools.enter_context(tc.tile_pool(name="keep", bufs=1))
        stage = pools.enter_context(tc.tile_pool(name="stage", bufs=3))
        accs = pools.enter_context(tc.tile_pool(name="accs", bufs=ACC_BUFS))
        psum = pools.enter_context(tc.psum_pool(name="psum", bufs=8))

        raw = {}
        codes = {}
        planes = {}
        for b in range(BATCH):
            for c in range(PASSES):
                raw[(b, c)] = keep.tile([P, PACK, N], BF16, name="raw%d%d" % (b, c))
                codes[(b, c)] = keep.tile([P, N], U32, name="codes%d%d" % (b, c), align_bytes=64)
                planes[(b, c)] = keep.tile([P, N], U8, name="planes%d%d" % (b, c), align_bytes=64)
        w3_cols = COUT // W3_CHUNKS
        wsc_cols = COUT // WSC_CHUNKS
        w3_words = [
            keep.tile([P, 2 * w3_cols], U8, name="w3_words%d" % i, align_bytes=64) for i in range(W3_CHUNKS)
        ]
        wsc_words = [
            keep.tile([P, X_GROUPS, 2 * wsc_cols], U8, name="wsc_words%d" % i, align_bytes=64)
            for i in range(WSC_CHUNKS)
        ]
        w3_plane = keep.tile([P, COUT], U8, name="w3_plane", align_bytes=64)
        wsc_planes = keep.tile([P, X_GROUPS, COUT], U8, name="wsc_planes", align_bytes=64)

        bn_rows = keep.tile([P, 2 * P], BF16, name="bn_rows")
        ident = keep.tile([P, P], BF16, name="ident")
        eps_col = keep.tile([P, 1], F32, name="eps_col")
        warm = keep.tile([P, 1], F32, name="warm")

        nc.vector.memset(bn_rows[64:P, :], 0.0)
        nc.vector.memset(eps_col[:], EPS)
        nc.vector.memset(w3_plane[:].bitcast(I32), 0)
        nc.vector.memset(wsc_planes[:].rearrange("p g n -> p (g n)").bitcast(I32), 0)
        nc.scalar.activation(out=warm[:], in_=eps_col[:], func=ACT.Abs_reciprocal_sqrt)

        bn_vectors = [bn3_v, scbn_v, bn3_g, scbn_g, bn3_m, scbn_m, bn3_b, scbn_b, sc_b]
        for v, vector in enumerate(bn_vectors):
            queue = nc.sync if v < 7 else nc.gpsimd
            queue.dma_start(out=bn_rows[8 * v : 8 * v + 8, :], in_=vector.rearrange("(r c) -> r c", c=2 * P))
        make_identity(nc, ident[:])

        def load_activations(queue, b):
            queue.dma_start(out=raw[(b, 0)][:], in_=h_attn[b].rearrange("(p t) n -> p t n", t=PACK))

        def load_x(queue, b):
            for g in range(X_GROUPS):
                queue.dma_start(
                    out=raw[(b, 1 + g)][:],
                    in_=x[b, 512 * g : 512 * (g + 1), :].rearrange("(p t) n -> p t n", t=PACK),
                )

        def load_w3(i):
            nc.sync.dma_start(
                out=w3_words[i][:].bitcast(I32),
                in_=conv3_w_words[0, :, 2 * w3_cols * i : 2 * w3_cols * (i + 1)].bitcast(I32),
            )

        def load_wsc(i):
            nc.sync.dma_start(
                out=wsc_words[i][:].bitcast(I32),
                in_=sc_w_words[:, :, 2 * wsc_cols * i : 2 * wsc_cols * (i + 1)]
                .rearrange("g p w -> p g w")
                .bitcast(I32),
            )

        load_activations(nc.scalar, 0)
        for q in range(4):
            nc.sync.dma_start(
                out=w3_plane[32 * q : 32 * q + 4, :].bitcast(I32),
                in_=conv3_w_scales[0, 4 * q : 4 * q + 4, :].bitcast(I32),
            )
        load_w3(0)
        load_x(nc.scalar, 0)
        load_wsc(0)
        for q in range(4):
            nc.sync.dma_start(
                out=wsc_planes[32 * q : 32 * q + 4, :, :].bitcast(I32),
                in_=sc_w_scales[:, 4 * q : 4 * q + 4, :].rearrange("g r n -> r g n").bitcast(I32),
            )
        load_w3(1)
        load_wsc(1)
        load_activations(nc.sync, 1)
        load_x(nc.sync, 1)
        load_wsc(2)
        load_wsc(3)

        bn_ps = psum.tile([P, 2, P], BF16, tag="bank", name="bn_ps")
        for h in range(2):
            nc.tensor.transpose(bn_ps[:, h, :], bn_rows[:, P * h : P * (h + 1)], ident[:])
        bn = keep.tile([P, 9, 8, 2], F32, name="bn")
        nc.scalar.copy(out=bn[:], in_=bn_ps[:, :, 0:72].rearrange("p h (v r) -> p v r h", v=9))
        by_tile = bn[:].rearrange("p v r h -> p v (r h)")
        rstd = keep.tile([P, 2, CO_TILES], F32, name="rstd")
        slope = keep.tile([P, 2, CO_TILES], F32, name="slope")
        shift = keep.tile([P, CO_TILES], F32, name="shift")
        nc.scalar.activation(out=rstd[:], in_=by_tile[:, 0:2, :], func=ACT.Abs_reciprocal_sqrt, bias=eps_col[:, 0:1])
        nc.gpsimd.tensor_sub(out=by_tile[:, 5, :], in0=by_tile[:, 8, :], in1=by_tile[:, 5, :])
        nc.gpsimd.tensor_add(out=by_tile[:, 6, :], in0=by_tile[:, 6, :], in1=by_tile[:, 7, :])
        nc.gpsimd.tensor_mul(out=slope[:], in0=by_tile[:, 2:4, :], in1=rstd[:])
        nc.gpsimd.tensor_mul(out=by_tile[:, 4:6, :], in0=by_tile[:, 4:6, :], in1=slope[:])
        nc.gpsimd.tensor_sub(out=by_tile[:, 6, :], in0=by_tile[:, 6, :], in1=by_tile[:, 4, :])
        nc.gpsimd.tensor_add(out=shift[:], in0=by_tile[:, 6, :], in1=by_tile[:, 5, :])

        grouped_of = {}

        def regroup(b, c):
            grouped = stage.tile([P, N, PACK], BF16, name="grouped", align_bytes=64)
            grouped_of[(b, c)] = grouped
            source = raw[(b, c)][:].rearrange("p t (c i) -> p c t i", i=4)
            target = grouped[:].rearrange("p (c i) t -> p c t i", i=4)
            split = (VECTOR_COLS if b == 0 else LATER_VECTOR_COLS) // 4
            nc.vector.tensor_copy(out=target[:, 0:split], in_=source[:, 0:split])
            nc.scalar.copy(out=target[:, split:], in_=source[:, split:])

        def quantise(b, c):
            nc.vector.quantize_mx(
                out=codes[(b, c)][:].bitcast(FP8X4),
                scales=planes[(b, c)][:],
                in_=grouped_of[(b, c)][:].rearrange("p n t -> p (n t)"),
            )

        for c in range(PASSES):
            regroup(0, c)
            quantise(0, c)
        later = {1: (regroup, 0), 2: (quantise, 0), 5: (regroup, 1), 6: (quantise, 1), 9: (regroup, 2), 10: (quantise, 2)}

        tiles = [(b, ct) for b in range(BATCH) for ct in range(CO_TILES)]
        count = len(tiles)
        acc_of = {}

        def main_tile(i):
            b, ct = tiles[i]
            if ct % 2 == 0:
                acc_of[(b, ct // 2)] = accs.tile([P, 2, N], F32, name="acc")
            acc = acc_of[(b, ct // 2)]
            chunk, col = divmod(ct * P, w3_cols)
            main = psum.tile([P, N], F32, tag="bank", name="main")
            nc.tensor.matmul_mx(
                out=main[:],
                lhsT=w3_words[chunk][:, 2 * col : 2 * (col + P)].bitcast(FP4X4),
                lhsT_scale=w3_plane[:, ct * P : (ct + 1) * P],
                rhs=codes[(b, 0)][:].bitcast(FP8X4),
                rhs_scale=planes[(b, 0)][:],
                start=True,
                stop=True,
            )
            if i < LEAD and i % 2 == 1:
                nc.vector.tensor_scalar(
                    out=acc[:, ct % 2, :],
                    in0=main[:],
                    scalar1=slope[:, 0, ct : ct + 1],
                    scalar2=shift[:, ct : ct + 1],
                    op0=ALU.mult,
                    op1=ALU.add,
                )
            else:
                nc.scalar.activation(
                    out=acc[:, ct % 2, :],
                    in_=main[:],
                    func=ACT.Identity,
                    scale=slope[:, 0, ct : ct + 1],
                    bias=shift[:, ct : ct + 1],
                )

        def short_tile(i):
            b, ct = tiles[i]
            acc = acc_of[(b, ct // 2)]
            chunk, col = divmod(ct * P, wsc_cols)
            short = psum.tile([P, N], F32, tag="bank", name="short")
            for g in range(X_GROUPS):
                nc.tensor.matmul_mx(
                    out=short[:],
                    lhsT=wsc_words[chunk][:, g, 2 * col : 2 * (col + P)].bitcast(FP4X4),
                    lhsT_scale=wsc_planes[:, g, ct * P : (ct + 1) * P],
                    rhs=codes[(b, 1 + g)][:].bitcast(FP8X4),
                    rhs_scale=planes[(b, 1 + g)][:],
                    start=(g == 0),
                    stop=(g == X_GROUPS - 1),
                )
            nc.vector.scalar_tensor_tensor(
                out=acc[:, ct % 2, :],
                in0=short[:],
                scalar=slope[:, 1, ct : ct + 1],
                in1=acc[:, ct % 2, :],
                op0=ALU.mult,
                op1=ALU.add,
            )
            if i >= count - SINGLES:
                if i == count - 1:
                    nc.vector.tensor_scalar_max(out=acc[:, ct % 2, :], in0=acc[:, ct % 2, :], scalar1=0.0)
                elif i == count - 2:
                    nc.scalar.activation(out=acc[:, ct % 2, :], in_=acc[:, ct % 2, :], func=ACT.Relu)
                else:
                    nc.gpsimd.tensor_scalar(
                        out=acc[:, ct % 2, :], in0=acc[:, ct % 2, :], scalar1=FLT_MAX, scalar2=0.0, op0=ALU.min, op1=ALU.max
                    )
                nc.sync.dma_start(out=out[b, ct * P : (ct + 1) * P, :], in_=acc[:, ct % 2, :])
            elif i < SHORT_RELUS:
                nc.gpsimd.tensor_scalar(
                    out=acc[:, ct % 2, :], in0=acc[:, ct % 2, :], scalar1=FLT_MAX, scalar2=0.0, op0=ALU.min, op1=ALU.max
                )
                if ct % 2 == 1:
                    nc.sync.dma_start(
                        out=out[b, (ct - 1) * P : (ct + 1) * P, :].rearrange("(j p) n -> p j n", p=P),
                        in_=acc[:],
                    )
            elif ct % 2 == 1:
                nc.gpsimd.tensor_scalar(
                    out=acc[:], in0=acc[:], scalar1=FLT_MAX, scalar2=0.0, op0=ALU.min, op1=ALU.max
                )
                nc.sync.dma_start(
                    out=out[b, (ct - 1) * P : (ct + 1) * P, :].rearrange("(j p) n -> p j n", p=P),
                    in_=acc[:],
                )

        issued = 0
        for s in range(count):
            if s in later:
                later[s][0](1, later[s][1])
            lead = 2 + ((LEAD - 2) * (count - 1 - s)) // (count - 1)
            while issued < min(count, s + lead):
                main_tile(issued)
                issued += 1
            short_tile(s)
